import numpy as np
import ml_dtypes


def mxq(x, axis, fmt="e4m3"):
    dtype, down = {"e4m3": (ml_dtypes.float8_e4m3fn, 7), "e5m2": (ml_dtypes.float8_e5m2, 14)}[fmt]
    v = np.moveaxis(np.asarray(x, np.float32).astype(ml_dtypes.bfloat16).astype(np.float64), axis, -1)
    blocks = v.reshape(v.shape[:-1] + (-1, 32))
    amax = np.abs(blocks).max(-1, keepdims=True)
    byte = np.maximum(np.where(amax > 0, np.frexp(amax)[1] - 1 + 127, 0) - down, 1)
    scale = np.exp2(byte - 127.0)
    codes = (blocks / scale).astype(np.float32).astype(dtype).astype(np.float64)
    return np.moveaxis((codes * scale).reshape(v.shape), -1, axis)


WIDE = False


def mx_kscale(k):
    if not WIDE:
        return np.ones(k)
    levels = np.array([10, -10, 5, -5, 0])
    a = np.random.permutation(np.resize(levels, k // 512 * 4)).reshape(k // 512, 4)
    idx = np.arange(k)
    return np.exp2(a[idx // 512, idx % 128 // 32])


BF16 = ml_dtypes.bfloat16


def bf(x):
    return np.asarray(x, np.float32).astype(BF16)


def f64(x):
    return np.asarray(x).astype(np.float64)


B, T, HS, C, NH, HD, WS, MAXD = 1, 8, 28, 512, 32, 16, 7, 3
N = T * HS * HS
E = NH * HD
BT = B * NH * T
EPS = 1e-12


def l2norm(v, axis):
    return v / np.maximum(np.sqrt(np.sum(v * v, axis=axis, keepdims=True)), EPS)


def setup_inputs():
    s = mx_kscale(C)
    return {"x": bf(np.random.standard_normal((B, N, C)) * s),
            "q_w": bf(np.random.standard_normal((E, C)) / np.sqrt(C) / s),
            "k_w": bf(np.random.standard_normal((E, C)) / np.sqrt(C) / s)}


def reference(x, q_w, k_w):
    xq = mxq(f64(x), 2, "e4m3")
    q = xq @ mxq(f64(q_w), 1, "e4m3").T
    k = xq @ mxq(f64(k_w), 1, "e4m3").T
    q = q.reshape(B, N, NH, HD).transpose(0, 2, 1, 3)
    k = k.reshape(B, N, NH, HD).transpose(0, 2, 1, 3)
    q = q.reshape(B * NH, T, HS, HS, HD).transpose(0, 1, 4, 2, 3)
    k = k.reshape(B * NH, T, HS, HS, HD).transpose(0, 1, 4, 2, 3)
    k_post = np.concatenate([k[:, 1:], k[:, -1:]], axis=1)
    qp = l2norm(q.reshape(BT, HD, HS, HS), 1)
    kp = l2norm(k_post.reshape(BT, HD, HS, HS), 1)
    return qp, kp

@@ -1,0 +1,228 @@
+from contextlib import ExitStack
+
+import concourse.mybir as mybir
+from concourse.masks import make_identity
+
+F32 = mybir.dt.float32
+BF16 = mybir.dt.bfloat16
+U32 = mybir.dt.uint32
+U8 = mybir.dt.uint8
+FP8X4 = mybir.dt.float8_e4m3fn_x4
+ALU = mybir.AluOpType
+ACT = mybir.ActivationFunctionType
+
+P = 128
+PACK = 4
+HALVES = 2
+C = 512
+T = 8
+FRAME = 784
+TOKENS = T * FRAME
+HEADS = 32
+D_LO = 4
+D_HI = 4
+UNIT = 128
+UNITS = TOKENS // UNIT
+BLOCK = 4
+BLOCKS = (UNITS + BLOCK - 1) // BLOCK
+FIRST_KEY_UNIT = FRAME // UNIT
+BANK_ROWS = 2
+MAX_INV_NORM = 1.0e12
+LAG_SUM = 2
+LAG_NORM = 3
+LAG_SCALE = 4
+AHEAD = 8
+
+FLOPS = 2 * TOKENS * C * (2 * HEADS * D_LO * D_HI)
+
+
+def turn_rows(nc, banks, stage, identity, rows):
+    groups = rows.shape[1]
+    grouped = stage.tile([P, BLOCK * P * PACK], BF16, align_bytes=64)
+    grouped_words = grouped[:].bitcast(F32).rearrange("p (g r u) -> p g r u", r=P, u=HALVES)
+    for first in range(0, groups, BANK_ROWS):
+        count = min(BANK_ROWS, groups - first)
+        turned = banks.tile([P, BANK_ROWS, HALVES, P], F32, tag="bank")
+        for g in range(count):
+            row_words = rows[:, first + g, :].bitcast(F32)
+            for u in range(HALVES):
+                nc.tensor.transpose(turned[:, g, u, :], row_words[:, u * P : (u + 1) * P], identity[:])
+        copy_out = nc.vector.tensor_copy if (first // BANK_ROWS) % 2 == 0 else nc.scalar.copy
+        copy_out(
+            grouped_words[:, first : first + count],
+            turned[:, 0:count].rearrange("p g u r -> p g r u"),
+        )
+    return grouped[:, 0 : groups * P * PACK]
+
+
+def quantise(nc, grouped, codes, scales):
+    nc.vector.quantize_mx(out=codes.bitcast(FP8X4), scales=scales, in_=grouped)
+
+
+def frame_pieces(unit):
+    start = unit * UNIT
+    end = start + UNIT
+    return [
+        (frame, max(start, frame * FRAME), min(end, (frame + 1) * FRAME))
+        for frame in range(start // FRAME, (end - 1) // FRAME + 1)
+    ]
+
+
+def frames_fed(shift, frame):
+    return [t for t in range(T) if min(t + shift, T - 1) == frame]
+
+
+def tile_costvolumeattention17_pa_kernel(tc, x, q_w, k_w, out_0, out_1):
+    nc = tc.nc
+    with ExitStack() as ctx:
+        keep = ctx.enter_context(tc.tile_pool(name="keep", bufs=1))
+        loads = ctx.enter_context(tc.tile_pool(name="loads", bufs=BLOCKS))
+        stage = ctx.enter_context(tc.tile_pool(name="stage", bufs=3))
+        norm = ctx.enter_context(tc.tile_pool(name="norm", bufs=8))
+        frames = ctx.enter_context(tc.tile_pool(name="frames", bufs=3))
+        banks = ctx.enter_context(tc.psum_pool(name="banks", bufs=8))
+        ctx.enter_context(tc.manual_schedule())
+
+        w_codes = {}
+        w_scales = {}
+        for name in ("q", "k"):
+            w_codes[name] = keep.tile([P, D_HI * P], U32, align_bytes=64, name="w_codes_" + name)
+            w_scales[name] = keep.tile([P, D_HI * P], U8, align_bytes=64, name="w_scales_" + name)
+        x_codes = keep.tile([P, TOKENS], U32, align_bytes=64)
+        x_scales = keep.tile([P, TOKENS], U8, align_bytes=64)
+
+        x_rows = x[0].rearrange("(a p) c -> p a c", p=P)
+        weights = (("q", q_w, 0), ("k", k_w, FIRST_KEY_UNIT))
+        jobs = []
+        for block in range(BLOCKS):
+            first = block * BLOCK
+            count = min(BLOCK, UNITS - first)
+            x_block = loads.tile([P, count, C], BF16, tag="x_block")
+            nc.sync.dma_start(out=x_block[:], in_=x_rows[:, first : first + count, :])
+            columns = slice(first * UNIT, (first + count) * UNIT)
+            jobs.append((x_block, x_codes[:, columns], x_scales[:, columns], first))
+            for name, w, first_use in weights[block : block + 1]:
+                w_rows = keep.tile([P, D_HI, C], BF16, name="w_rows_" + name)
+                nc.sync.dma_start(out=w_rows[:], in_=w.rearrange("(m j) c -> m j c", j=D_HI))
+                jobs.append((w_rows, w_codes[name][:], w_scales[name][:], first_use))
+
+        identity = keep.tile([P, P], F32)
+        make_identity(nc, identity[:])
+        same_head = keep.tile([P, HEADS], F32)
+        nc.vector.tensor_reduce(
+            out=same_head[:],
+            in_=identity[:].rearrange("p (h i) -> p h i", i=D_LO),
+            axis=mybir.AxisListType.X,
+            op=ALU.add,
+        )
+        ones_lo = keep.tile([P, HEADS, D_LO], F32)
+        nc.vector.tensor_copy(out=ones_lo[:], in_=same_head[:].unsqueeze(2).to_broadcast([P, HEADS, D_LO]))
+
+        outputs = {
+            "q": out_0.rearrange("(h t) (dlo dhi) i j -> t dlo h (dhi i j)", t=T, dlo=D_LO),
+            "k": out_1.rearrange("(h t) (dlo dhi) i j -> t dlo h (dhi i j)", t=T, dlo=D_LO),
+        }
+        shifts = {"q": 0, "k": 1}
+
+        items = []
+        for last_frame in range(T):
+            for name in ("k", "q"):
+                for unit in range(UNITS):
+                    pieces = [piece for piece in frame_pieces(unit) if frames_fed(shifts[name], piece[0])]
+                    if pieces and frame_pieces(unit)[-1][0] == last_frame:
+                        items.append((unit, name, pieces))
+
+        products = {}
+        squares = {}
+        pair_sums = {}
+        hi_sums = {}
+        inv_norms = {}
+        frame_tiles = {}
+
+        def multiply(i):
+            unit, name, pieces = items[i]
+            tokens = slice(unit * UNIT, (unit + 1) * UNIT)
+            products[i] = banks.tile([P, D_HI, UNIT], F32, tag="bank", name="product")
+            for j in range(D_HI):
+                nc.tensor.matmul_mx(
+                    out=products[i][:, j, :],
+                    lhsT=w_codes[name][:, j * P : (j + 1) * P].bitcast(FP8X4),
+                    lhsT_scale=w_scales[name][:, j * P : (j + 1) * P],
+                    rhs=x_codes[:, tokens].bitcast(FP8X4),
+                    rhs_scale=x_scales[:, tokens],
+                    start=True,
+                    stop=True,
+                )
+            squares[i] = norm.tile([P, D_HI, UNIT], F32, name="squares")
+            nc.scalar.activation(out=squares[i][:], in_=products[i][:], func=ACT.Square)
+            pair_sums[i] = norm.tile([P, D_HI // 2, UNIT], F32, name="pair_sums")
+            nc.gpsimd.tensor_tensor(
+                out=pair_sums[i][:], in0=squares[i][:, 0:2, :], in1=squares[i][:, 2:4, :], op=ALU.add
+            )
+
+        def finish_sum(i):
+            hi_sums[i] = norm.tile([P, UNIT], F32, name="hi_sums")
+            nc.vector.tensor_tensor(
+                out=hi_sums[i][:], in0=pair_sums[i][:, 0, :], in1=pair_sums[i][:, 1, :], op=ALU.add
+            )
+
+        def invert_norm(i):
+            head_sums = banks.tile([P, UNIT], F32, tag="bank")
+            nc.tensor.matmul(
+                out=head_sums[:],
+                lhsT=ones_lo[:].rearrange("p h i -> p (h i)"),
+                rhs=hi_sums[i][:],
+                start=True,
+                stop=True,
+            )
+            inv_norms[i] = norm.tile([P, UNIT], F32, name="inv_norm")
+            nc.scalar.activation(out=inv_norms[i][:], in_=head_sums[:], func=ACT.Abs_reciprocal_sqrt)
+
+        def scale_and_store(i):
+            unit, name, pieces = items[i]
+            for frame, start, end in pieces:
+                if start == frame * FRAME:
+                    frame_tiles[name] = frames.tile([P, D_HI, FRAME], F32, name="frame_" + name)
+                frame_tile = frame_tiles[name]
+                width = end - start
+                lo = start - unit * UNIT
+                nc.vector.scalar_tensor_tensor(
+                    out=frame_tile[:, :, start - frame * FRAME : end - frame * FRAME],
+                    in0=inv_norms[i][:, lo : lo + width].unsqueeze(1).to_broadcast([P, D_HI, width]),
+                    scalar=MAX_INV_NORM,
+                    in1=products[i][:, :, lo : lo + width],
+                    op0=ALU.min,
+                    op1=ALU.mult,
+                )
+                if end == (frame + 1) * FRAME:
+                    for t in frames_fed(shifts[name], frame):
+                        for d_lo in range(D_LO):
+                            nc.sync.dma_start(
+                                out=outputs[name][t, d_lo],
+                                in_=frame_tile[d_lo:P:D_LO].rearrange("p j n -> p (j n)"),
+                            )
+
+        at_once = [job for job in jobs if job[3] == 0]
+        turned_rows = [turn_rows(nc, banks, stage, identity, job[0]) for job in at_once]
+        for job, grouped in zip(at_once, turned_rows):
+            quantise(nc, grouped, job[1], job[2])
+        later = [job for job in jobs if job[3] > 0]
+
+        waiting = []
+        next_job = 0
+        for step in range(len(items) + LAG_SCALE):
+            if step < len(items):
+                for job, grouped in waiting:
+                    quantise(nc, grouped, job[1], job[2])
+                waiting = []
+                if next_job < len(later) and later[next_job][3] <= items[step][0] + AHEAD:
+                    job = later[next_job]
+                    next_job += 1
+                    waiting = [(job, turn_rows(nc, banks, stage, identity, job[0]))]
+                multiply(step)
+            if 0 <= step - LAG_SUM < len(items):
+                finish_sum(step - LAG_SUM)
+            if 0 <= step - LAG_NORM < len(items):
+                invert_norm(step - LAG_NORM)
+            if 0 <= step - LAG_SCALE < len(items):
+                scale_and_store(step - LAG_SCALE)

@@ -21,47 +21,47 @@ TOKENS = T * FRAME
 HEADS = 32
 D_LO = 4
 D_HI = 4
-UNIT = 128
-UNITS = TOKENS // UNIT
+GROUP = 256
+GROUPS = (TOKENS + GROUP - 1) // GROUP
+BANK_HI = 2
 BLOCK = 4
-BLOCKS = (UNITS + BLOCK - 1) // BLOCK
-FIRST_KEY_UNIT = FRAME // UNIT
+BLOCK_TOKENS = BLOCK * P
+BLOCKS = (TOKENS + BLOCK_TOKENS - 1) // BLOCK_TOKENS
 BANK_ROWS = 2
 MAX_INV_NORM = 1.0e12
 LAG_SUM = 2
 LAG_NORM = 3
 LAG_SCALE = 4
-AHEAD = 8
+AHEAD = 4 * GROUP
 
 FLOPS = 2 * TOKENS * C * (2 * HEADS * D_LO * D_HI)
 
 
 def turn_rows(nc, banks, stage, identity, rows):
-    groups = rows.shape[1]
+    sets = rows.shape[1]
     grouped = stage.tile([P, BLOCK * P * PACK], BF16, align_bytes=64)
     grouped_words = grouped[:].bitcast(F32).rearrange("p (g r u) -> p g r u", r=P, u=HALVES)
-    for first in range(0, groups, BANK_ROWS):
-        count = min(BANK_ROWS, groups - first)
+    for first in range(0, sets, BANK_ROWS):
+        count = min(BANK_ROWS, sets - first)
         turned = banks.tile([P, BANK_ROWS, HALVES, P], F32, tag="bank")
         for g in range(count):
             row_words = rows[:, first + g, :].bitcast(F32)
             for u in range(HALVES):
                 nc.tensor.transpose(turned[:, g, u, :], row_words[:, u * P : (u + 1) * P], identity[:])
-        copy_out = nc.vector.tensor_copy if (first // BANK_ROWS) % 2 == 0 else nc.scalar.copy
-        copy_out(
+        nc.scalar.copy(
             grouped_words[:, first : first + count],
             turned[:, 0:count].rearrange("p g u r -> p g r u"),
         )
-    return grouped[:, 0 : groups * P * PACK]
+    return grouped[:, 0 : sets * P * PACK]
 
 
 def quantise(nc, grouped, codes, scales):
     nc.vector.quantize_mx(out=codes.bitcast(FP8X4), scales=scales, in_=grouped)
 
 
-def frame_pieces(unit):
-    start = unit * UNIT
-    end = start + UNIT
+def frame_pieces(group):
+    start = group * GROUP
+    end = min(start + GROUP, TOKENS)
     return [
         (frame, max(start, frame * FRAME), min(end, (frame + 1) * FRAME))
         for frame in range(start // FRAME, (end - 1) // FRAME + 1)
@@ -78,7 +78,7 @@ def tile_costvolumeattention17_pa_kernel(tc, x, q_w, k_w, out_0, out_1):
         keep = ctx.enter_context(tc.tile_pool(name="keep", bufs=1))
         loads = ctx.enter_context(tc.tile_pool(name="loads", bufs=BLOCKS))
         stage = ctx.enter_context(tc.tile_pool(name="stage", bufs=3))
-        norm = ctx.enter_context(tc.tile_pool(name="norm", bufs=8))
+        norm = ctx.enter_context(tc.tile_pool(name="norm", bufs=4))
         frames = ctx.enter_context(tc.tile_pool(name="frames", bufs=3))
         banks = ctx.enter_context(tc.psum_pool(name="banks", bufs=8))
         ctx.enter_context(tc.manual_schedule())
@@ -91,20 +91,35 @@ def tile_costvolumeattention17_pa_kernel(tc, x, q_w, k_w, out_0, out_1):
         x_codes = keep.tile([P, TOKENS], U32, align_bytes=64)
         x_scales = keep.tile([P, TOKENS], U8, align_bytes=64)
 
+        outputs = {
+            "q": out_0.rearrange("(h t) (dlo dhi) i j -> t dlo h dhi (i j)", t=T, dlo=D_LO),
+            "k": out_1.rearrange("(h t) (dlo dhi) i j -> t dlo h dhi (i j)", t=T, dlo=D_LO),
+        }
+        shifts = {"q": 0, "k": 1}
+
+        items = []
+        for last_frame in range(T):
+            for name in ("k", "q"):
+                for group in range(GROUPS):
+                    pieces = [piece for piece in frame_pieces(group) if frames_fed(shifts[name], piece[0])]
+                    if pieces and frame_pieces(group)[-1][0] == last_frame:
+                        items.append((group, name, pieces))
+        first_use = {name: min([item[0] for item in items if item[1] == name]) * GROUP for name in ("q", "k")}
+
         x_rows = x[0].rearrange("(a p) c -> p a c", p=P)
-        weights = (("q", q_w, 0), ("k", k_w, FIRST_KEY_UNIT))
+        weights = (("q", q_w), ("k", k_w))
         jobs = []
         for block in range(BLOCKS):
             first = block * BLOCK
-            count = min(BLOCK, UNITS - first)
+            count = min(BLOCK, TOKENS // P - first)
             x_block = loads.tile([P, count, C], BF16, tag="x_block")
             nc.sync.dma_start(out=x_block[:], in_=x_rows[:, first : first + count, :])
-            columns = slice(first * UNIT, (first + count) * UNIT)
-            jobs.append((x_block, x_codes[:, columns], x_scales[:, columns], first))
-            for name, w, first_use in weights[block : block + 1]:
+            columns = slice(first * P, (first + count) * P)
+            jobs.append((x_block, x_codes[:, columns], x_scales[:, columns], first * P))
+            for name, w in weights[block : block + 1]:
                 w_rows = keep.tile([P, D_HI, C], BF16, name="w_rows_" + name)
                 nc.sync.dma_start(out=w_rows[:], in_=w.rearrange("(m j) c -> m j c", j=D_HI))
-                jobs.append((w_rows, w_codes[name][:], w_scales[name][:], first_use))
+                jobs.append((w_rows, w_codes[name][:], w_scales[name][:], first_use[name]))
 
         identity = keep.tile([P, P], F32)
         make_identity(nc, identity[:])
@@ -118,89 +133,107 @@ def tile_costvolumeattention17_pa_kernel(tc, x, q_w, k_w, out_0, out_1):
         ones_lo = keep.tile([P, HEADS, D_LO], F32)
         nc.vector.tensor_copy(out=ones_lo[:], in_=same_head[:].unsqueeze(2).to_broadcast([P, HEADS, D_LO]))
 
-        outputs = {
-            "q": out_0.rearrange("(h t) (dlo dhi) i j -> t dlo h (dhi i j)", t=T, dlo=D_LO),
-            "k": out_1.rearrange("(h t) (dlo dhi) i j -> t dlo h (dhi i j)", t=T, dlo=D_LO),
-        }
-        shifts = {"q": 0, "k": 1}
-
-        items = []
-        for last_frame in range(T):
-            for name in ("k", "q"):
-                for unit in range(UNITS):
-                    pieces = [piece for piece in frame_pieces(unit) if frames_fed(shifts[name], piece[0])]
-                    if pieces and frame_pieces(unit)[-1][0] == last_frame:
-                        items.append((unit, name, pieces))
-
-        products = {}
-        squares = {}
         pair_sums = {}
         hi_sums = {}
         inv_norms = {}
         frame_tiles = {}
 
-        def multiply(i):
-            unit, name, pieces = items[i]
-            tokens = slice(unit * UNIT, (unit + 1) * UNIT)
-            products[i] = banks.tile([P, D_HI, UNIT], F32, tag="bank", name="product")
-            for j in range(D_HI):
+        def width_of(i):
+            return min(GROUP, TOKENS - items[i][0] * GROUP)
+
+        def multiply(i, first_hi):
+            group, name, pieces = items[i]
+            tokens = slice(group * GROUP, group * GROUP + width_of(i))
+            product = banks.tile([P, BANK_HI, GROUP], F32, tag="bank")
+            for j in range(BANK_HI):
+                channels = slice((first_hi + j) * P, (first_hi + j + 1) * P)
                 nc.tensor.matmul_mx(
-                    out=products[i][:, j, :],
-                    lhsT=w_codes[name][:, j * P : (j + 1) * P].bitcast(FP8X4),
-                    lhsT_scale=w_scales[name][:, j * P : (j + 1) * P],
+                    out=product[:, j, 0 : width_of(i)],
+                    lhsT=w_codes[name][:, channels].bitcast(FP8X4),
+                    lhsT_scale=w_scales[name][:, channels],
                     rhs=x_codes[:, tokens].bitcast(FP8X4),
                     rhs_scale=x_scales[:, tokens],
                     start=True,
                     stop=True,
                 )
-            squares[i] = norm.tile([P, D_HI, UNIT], F32, name="squares")
-            nc.scalar.activation(out=squares[i][:], in_=products[i][:], func=ACT.Square)
-            pair_sums[i] = norm.tile([P, D_HI // 2, UNIT], F32, name="pair_sums")
+            return product
+
+        def square(i):
+            width = width_of(i)
+            squares = norm.tile([P, D_HI, GROUP], F32)
+            for first_hi in range(0, D_HI, BANK_HI):
+                product = multiply(i, first_hi)
+                nc.scalar.activation(
+                    out=squares[:, first_hi : first_hi + BANK_HI, 0:width],
+                    in_=product[:, :, 0:width],
+                    func=ACT.Square,
+                )
+            pair_sums[i] = norm.tile([P, D_HI // 2, GROUP], F32, name="pair_sums")
             nc.gpsimd.tensor_tensor(
-                out=pair_sums[i][:], in0=squares[i][:, 0:2, :], in1=squares[i][:, 2:4, :], op=ALU.add
+                out=pair_sums[i][:, :, 0:width],
+                in0=squares[:, 0:2, 0:width],
+                in1=squares[:, 2:4, 0:width],
+                op=ALU.add,
             )
 
         def finish_sum(i):
-            hi_sums[i] = norm.tile([P, UNIT], F32, name="hi_sums")
+            width = width_of(i)
+            hi_sums[i] = norm.tile([P, GROUP], F32, name="hi_sums")
             nc.vector.tensor_tensor(
-                out=hi_sums[i][:], in0=pair_sums[i][:, 0, :], in1=pair_sums[i][:, 1, :], op=ALU.add
+                out=hi_sums[i][:, 0:width],
+                in0=pair_sums[i][:, 0, 0:width],
+                in1=pair_sums[i][:, 1, 0:width],
+                op=ALU.add,
             )
 
         def invert_norm(i):
-            head_sums = banks.tile([P, UNIT], F32, tag="bank")
+            width = width_of(i)
+            head_sums = banks.tile([P, GROUP], F32, tag="bank")
             nc.tensor.matmul(
-                out=head_sums[:],
+                out=head_sums[:, 0:width],
                 lhsT=ones_lo[:].rearrange("p h i -> p (h i)"),
-                rhs=hi_sums[i][:],
+                rhs=hi_sums[i][:, 0:width],
                 start=True,
                 stop=True,
             )
-            inv_norms[i] = norm.tile([P, UNIT], F32, name="inv_norm")
-            nc.scalar.activation(out=inv_norms[i][:], in_=head_sums[:], func=ACT.Abs_reciprocal_sqrt)
+            inv_norms[i] = norm.tile([P, GROUP], F32, name="inv_norm")
+            nc.scalar.activation(
+                out=inv_norms[i][:, 0:width], in_=head_sums[:, 0:width], func=ACT.Abs_reciprocal_sqrt
+            )
+
+        def store(name, frame, frame_tile, first, end):
+            for t in frames_fed(shifts[name], frame):
+                for d_lo in range(D_LO):
+                    nc.sync.dma_start(
+                        out=outputs[name][t, d_lo][:, :, first:end],
+                        in_=frame_tile[d_lo:P:D_LO, :, first:end],
+                    )
 
         def scale_and_store(i):
-            unit, name, pieces = items[i]
-            for frame, start, end in pieces:
-                if start == frame * FRAME:
-                    frame_tiles[name] = frames.tile([P, D_HI, FRAME], F32, name="frame_" + name)
-                frame_tile = frame_tiles[name]
-                width = end - start
-                lo = start - unit * UNIT
-                nc.vector.scalar_tensor_tensor(
-                    out=frame_tile[:, :, start - frame * FRAME : end - frame * FRAME],
-                    in0=inv_norms[i][:, lo : lo + width].unsqueeze(1).to_broadcast([P, D_HI, width]),
-                    scalar=MAX_INV_NORM,
-                    in1=products[i][:, :, lo : lo + width],
-                    op0=ALU.min,
-                    op1=ALU.mult,
-                )
+            group, name, pieces = items[i]
+            if pieces[0][1] == pieces[0][0] * FRAME:
+                frame_tiles[name] = [frames.tile([P, D_HI, FRAME], F32, name="frame_" + name)]
+            if len(pieces) > 1:
+                frame_tiles[name].append(frames.tile([P, D_HI, FRAME], F32, name="frame_" + name))
+            for first_hi in range(0, D_HI, BANK_HI):
+                product = multiply(i, first_hi)
+                for frame_tile, (frame, start, end) in zip(frame_tiles[name], pieces):
+                    columns = slice(start - group * GROUP, end - group * GROUP)
+                    nc.vector.scalar_tensor_tensor(
+                        out=frame_tile[:, first_hi : first_hi + BANK_HI, start - frame * FRAME : end - frame * FRAME],
+                        in0=inv_norms[i][:, columns].unsqueeze(1).to_broadcast([P, BANK_HI, end - start]),
+                        scalar=MAX_INV_NORM,
+                        in1=product[:, :, columns],
+                        op0=ALU.min,
+                        op1=ALU.mult,
+                    )
+            for frame_tile, (frame, start, end) in zip(list(frame_tiles[name]), pieces):
+                if frame == T - 1:
+                    store(name, frame, frame_tile, start - frame * FRAME, end - frame * FRAME)
+                elif end == (frame + 1) * FRAME:
+                    store(name, frame, frame_tile, 0, FRAME)
                 if end == (frame + 1) * FRAME:
-                    for t in frames_fed(shifts[name], frame):
-                        for d_lo in range(D_LO):
-                            nc.sync.dma_start(
-                                out=outputs[name][t, d_lo],
-                                in_=frame_tile[d_lo:P:D_LO].rearrange("p j n -> p (j n)"),
-                            )
+                    frame_tiles[name] = frame_tiles[name][1:]
 
         at_once = [job for job in jobs if job[3] == 0]
         turned_rows = [turn_rows(nc, banks, stage, identity, job[0]) for job in at_once]
@@ -215,11 +248,11 @@ def tile_costvolumeattention17_pa_kernel(tc, x, q_w, k_w, out_0, out_1):
                 for job, grouped in waiting:
                     quantise(nc, grouped, job[1], job[2])
                 waiting = []
-                if next_job < len(later) and later[next_job][3] <= items[step][0] + AHEAD:
+                if next_job < len(later) and later[next_job][3] <= items[step][0] * GROUP + AHEAD:
                     job = later[next_job]
                     next_job += 1
                     waiting = [(job, turn_rows(nc, banks, stage, identity, job[0]))]
-                multiply(step)
+                square(step)
             if 0 <= step - LAG_SUM < len(items):
                 finish_sum(step - LAG_SUM)
             if 0 <= step - LAG_NORM < len(items):

@@ -29,10 +29,11 @@ BLOCK_TOKENS = BLOCK * P
 BLOCKS = (TOKENS + BLOCK_TOKENS - 1) // BLOCK_TOKENS
 BANK_ROWS = 2
 MAX_INV_NORM = 1.0e12
-LAG_SUM = 2
-LAG_NORM = 3
-LAG_SCALE = 4
-AHEAD = 4 * GROUP
+LAG_SUM = 3
+LAG_NORM = 5
+LAG_SCALE = 6
+AHEAD = 4
+KEY_LEAD = 2
 
 FLOPS = 2 * TOKENS * C * (2 * HEADS * D_LO * D_HI)
 
@@ -48,7 +49,8 @@ def turn_rows(nc, banks, stage, identity, rows):
             row_words = rows[:, first + g, :].bitcast(F32)
             for u in range(HALVES):
                 nc.tensor.transpose(turned[:, g, u, :], row_words[:, u * P : (u + 1) * P], identity[:])
-        nc.scalar.copy(
+        copy_out = nc.vector.tensor_copy if (first // BANK_ROWS) % 2 == 0 else nc.scalar.copy
+        copy_out(
             grouped_words[:, first : first + count],
             turned[:, 0:count].rearrange("p g u r -> p g r u"),
         )
@@ -92,34 +94,38 @@ def tile_costvolumeattention17_pa_kernel(tc, x, q_w, k_w, out_0, out_1):
         x_scales = keep.tile([P, TOKENS], U8, align_bytes=64)
 
         outputs = {
-            "q": out_0.rearrange("(h t) (dlo dhi) i j -> t dlo h dhi (i j)", t=T, dlo=D_LO),
-            "k": out_1.rearrange("(h t) (dlo dhi) i j -> t dlo h dhi (i j)", t=T, dlo=D_LO),
+            "q": out_0.rearrange("(h t) (dlo dhi) i j -> t h dlo (dhi i j)", t=T, dlo=D_LO),
+            "k": out_1.rearrange("(h t) (dlo dhi) i j -> t h dlo (dhi i j)", t=T, dlo=D_LO),
         }
         shifts = {"q": 0, "k": 1}
 
         items = []
-        for last_frame in range(T):
-            for name in ("k", "q"):
+        for last_frame in range(-KEY_LEAD, T):
+            for name, lead in (("q", 0), ("k", KEY_LEAD)):
                 for group in range(GROUPS):
                     pieces = [piece for piece in frame_pieces(group) if frames_fed(shifts[name], piece[0])]
-                    if pieces and frame_pieces(group)[-1][0] == last_frame:
+                    if pieces and frame_pieces(group)[-1][0] == last_frame + lead:
                         items.append((group, name, pieces))
-        first_use = {name: min([item[0] for item in items if item[1] == name]) * GROUP for name in ("q", "k")}
 
         x_rows = x[0].rearrange("(a p) c -> p a c", p=P)
-        weights = (("q", q_w), ("k", k_w))
+        weights = {"q": q_w, "k": k_w}
         jobs = []
-        for block in range(BLOCKS):
-            first = block * BLOCK
-            count = min(BLOCK, TOKENS // P - first)
-            x_block = loads.tile([P, count, C], BF16, tag="x_block")
-            nc.sync.dma_start(out=x_block[:], in_=x_rows[:, first : first + count, :])
-            columns = slice(first * P, (first + count) * P)
-            jobs.append((x_block, x_codes[:, columns], x_scales[:, columns], first * P))
-            for name, w in weights[block : block + 1]:
+        seen = []
+        for i, (group, name, pieces) in enumerate(items):
+            if name not in seen:
+                seen.append(name)
                 w_rows = keep.tile([P, D_HI, C], BF16, name="w_rows_" + name)
-                nc.sync.dma_start(out=w_rows[:], in_=w.rearrange("(m j) c -> m j c", j=D_HI))
-                jobs.append((w_rows, w_codes[name][:], w_scales[name][:], first_use[name]))
+                nc.sync.dma_start(out=w_rows[:], in_=weights[name].rearrange("(m j) c -> m j c", j=D_HI))
+                jobs.append((w_rows, w_codes[name][:], w_scales[name][:], i))
+            block = group * GROUP // BLOCK_TOKENS
+            if block not in seen:
+                seen.append(block)
+                first = block * BLOCK
+                count = min(BLOCK, TOKENS // P - first)
+                x_block = loads.tile([P, count, C], BF16, tag="x_block")
+                nc.sync.dma_start(out=x_block[:], in_=x_rows[:, first : first + count, :])
+                columns = slice(first * P, (first + count) * P)
+                jobs.append((x_block, x_codes[:, columns], x_scales[:, columns], i))
 
         identity = keep.tile([P, P], F32)
         make_identity(nc, identity[:])
@@ -160,7 +166,7 @@ def tile_costvolumeattention17_pa_kernel(tc, x, q_w, k_w, out_0, out_1):
 
         def square(i):
             width = width_of(i)
-            squares = norm.tile([P, D_HI, GROUP], F32)
+            squares = norm.tile([P, D_HI, GROUP], F32, bufs=3)
             for first_hi in range(0, D_HI, BANK_HI):
                 product = multiply(i, first_hi)
                 nc.scalar.activation(
@@ -168,7 +174,7 @@ def tile_costvolumeattention17_pa_kernel(tc, x, q_w, k_w, out_0, out_1):
                     in_=product[:, :, 0:width],
                     func=ACT.Square,
                 )
-            pair_sums[i] = norm.tile([P, D_HI // 2, GROUP], F32, name="pair_sums")
+            pair_sums[i] = norm.tile([P, D_HI // 2, GROUP], F32, name="pair_sums", bufs=LAG_SUM + 2)
             nc.gpsimd.tensor_tensor(
                 out=pair_sums[i][:, :, 0:width],
                 in0=squares[:, 0:2, 0:width],
@@ -178,7 +184,7 @@ def tile_costvolumeattention17_pa_kernel(tc, x, q_w, k_w, out_0, out_1):
 
         def finish_sum(i):
             width = width_of(i)
-            hi_sums[i] = norm.tile([P, GROUP], F32, name="hi_sums")
+            hi_sums[i] = norm.tile([P, GROUP], F32, name="hi_sums", bufs=LAG_NORM - LAG_SUM + 2)
             nc.vector.tensor_tensor(
                 out=hi_sums[i][:, 0:width],
                 in0=pair_sums[i][:, 0, 0:width],
@@ -196,18 +202,17 @@ def tile_costvolumeattention17_pa_kernel(tc, x, q_w, k_w, out_0, out_1):
                 start=True,
                 stop=True,
             )
-            inv_norms[i] = norm.tile([P, GROUP], F32, name="inv_norm")
+            inv_norms[i] = norm.tile([P, GROUP], F32, name="inv_norm", bufs=LAG_SCALE - LAG_NORM + 2)
             nc.scalar.activation(
                 out=inv_norms[i][:, 0:width], in_=head_sums[:, 0:width], func=ACT.Abs_reciprocal_sqrt
             )
 
         def store(name, frame, frame_tile, first, end):
             for t in frames_fed(shifts[name], frame):
-                for d_lo in range(D_LO):
-                    nc.sync.dma_start(
-                        out=outputs[name][t, d_lo][:, :, first:end],
-                        in_=frame_tile[d_lo:P:D_LO, :, first:end],
-                    )
+                nc.sync.dma_start(
+                    out=outputs[name][t],
+                    in_=frame_tile[:].rearrange("p j n -> p (j n)"),
+                )
 
         def scale_and_store(i):
             group, name, pieces = items[i]
@@ -228,9 +233,7 @@ def tile_costvolumeattention17_pa_kernel(tc, x, q_w, k_w, out_0, out_1):
                         op1=ALU.mult,
                     )
             for frame_tile, (frame, start, end) in zip(list(frame_tiles[name]), pieces):
-                if frame == T - 1:
-                    store(name, frame, frame_tile, start - frame * FRAME, end - frame * FRAME)
-                elif end == (frame + 1) * FRAME:
+                if end == (frame + 1) * FRAME:
                     store(name, frame, frame_tile, 0, FRAME)
                 if end == (frame + 1) * FRAME:
                     frame_tiles[name] = frame_tiles[name][1:]
@@ -248,7 +251,7 @@ def tile_costvolumeattention17_pa_kernel(tc, x, q_w, k_w, out_0, out_1):
                 for job, grouped in waiting:
                     quantise(nc, grouped, job[1], job[2])
                 waiting = []
-                if next_job < len(later) and later[next_job][3] <= items[step][0] * GROUP + AHEAD:
+                if next_job < len(later) and later[next_job][3] <= step + AHEAD:
                     job = later[next_job]
                     next_job += 1
                     waiting = [(job, turn_rows(nc, banks, stage, identity, job[0]))]

@@ -33,7 +33,7 @@ LAG_SUM = 3
 LAG_NORM = 5
 LAG_SCALE = 6
 AHEAD = 4
-KEY_LEAD = 2
+KEY_LEAD = 3
 
 FLOPS = 2 * TOKENS * C * (2 * HEADS * D_LO * D_HI)
 
@@ -94,8 +94,8 @@ def tile_costvolumeattention17_pa_kernel(tc, x, q_w, k_w, out_0, out_1):
         x_scales = keep.tile([P, TOKENS], U8, align_bytes=64)
 
         outputs = {
-            "q": out_0.rearrange("(h t) (dlo dhi) i j -> t h dlo (dhi i j)", t=T, dlo=D_LO),
-            "k": out_1.rearrange("(h t) (dlo dhi) i j -> t h dlo (dhi i j)", t=T, dlo=D_LO),
+            "q": out_0.rearrange("(h t) (dlo dhi) i j -> t dhi h dlo (i j)", t=T, dlo=D_LO),
+            "k": out_1.rearrange("(h t) (dlo dhi) i j -> t dhi h dlo (i j)", t=T, dlo=D_LO),
         }
         shifts = {"q": 0, "k": 1}
 
@@ -209,10 +209,8 @@ def tile_costvolumeattention17_pa_kernel(tc, x, q_w, k_w, out_0, out_1):
 
         def store(name, frame, frame_tile, first, end):
             for t in frames_fed(shifts[name], frame):
-                nc.sync.dma_start(
-                    out=outputs[name][t],
-                    in_=frame_tile[:].rearrange("p j n -> p (j n)"),
-                )
+                for j in range(D_HI):
+                    nc.sync.dma_start(out=outputs[name][t, j][:, :, first:end], in_=frame_tile[:, j, first:end])
 
         def scale_and_store(i):
             group, name, pieces = items[i]
@@ -233,7 +231,9 @@ def tile_costvolumeattention17_pa_kernel(tc, x, q_w, k_w, out_0, out_1):
                         op1=ALU.mult,
                     )
             for frame_tile, (frame, start, end) in zip(list(frame_tiles[name]), pieces):
-                if end == (frame + 1) * FRAME:
+                if frame == T - 1:
+                    store(name, frame, frame_tile, start - frame * FRAME, end - frame * FRAME)
+                elif end == (frame + 1) * FRAME:
                     store(name, frame, frame_tile, 0, FRAME)
                 if end == (frame + 1) * FRAME:
                     frame_tiles[name] = frame_tiles[name][1:]

@@ -24,14 +24,16 @@ D_HI = 4
 GROUP = 256
 GROUPS = (TOKENS + GROUP - 1) // GROUP
 BANK_HI = 2
+BANK_SUMS = 2
 BLOCK = 4
 BLOCK_TOKENS = BLOCK * P
 BLOCKS = (TOKENS + BLOCK_TOKENS - 1) // BLOCK_TOKENS
 BANK_ROWS = 2
 MAX_INV_NORM = 1.0e12
-LAG_SUM = 3
-LAG_NORM = 5
+LAG_SUM = 2
+LAG_NORM = 4
 LAG_SCALE = 6
+BUNCH = 2
 AHEAD = 4
 KEY_LEAD = 3
 
@@ -94,8 +96,8 @@ def tile_costvolumeattention17_pa_kernel(tc, x, q_w, k_w, out_0, out_1):
         x_scales = keep.tile([P, TOKENS], U8, align_bytes=64)
 
         outputs = {
-            "q": out_0.rearrange("(h t) (dlo dhi) i j -> t dhi h dlo (i j)", t=T, dlo=D_LO),
-            "k": out_1.rearrange("(h t) (dlo dhi) i j -> t dhi h dlo (i j)", t=T, dlo=D_LO),
+            "q": out_0.rearrange("(h t) d i j -> t h d (i j)", t=T),
+            "k": out_1.rearrange("(h t) d i j -> t h d (i j)", t=T),
         }
         shifts = {"q": 0, "k": 1}
 
@@ -139,10 +141,11 @@ def tile_costvolumeattention17_pa_kernel(tc, x, q_w, k_w, out_0, out_1):
         ones_lo = keep.tile([P, HEADS, D_LO], F32)
         nc.vector.tensor_copy(out=ones_lo[:], in_=same_head[:].unsqueeze(2).to_broadcast([P, HEADS, D_LO]))
 
+        squares = {}
         pair_sums = {}
         hi_sums = {}
         inv_norms = {}
-        frame_tiles = {}
+        frame_tiles = {"q": [], "k": []}
 
         def width_of(i):
             return min(GROUP, TOKENS - items[i][0] * GROUP)
@@ -164,27 +167,30 @@ def tile_costvolumeattention17_pa_kernel(tc, x, q_w, k_w, out_0, out_1):
                 )
             return product
 
-        def square(i):
+        def square(i, first_hi):
             width = width_of(i)
-            squares = norm.tile([P, D_HI, GROUP], F32, bufs=3)
-            for first_hi in range(0, D_HI, BANK_HI):
-                product = multiply(i, first_hi)
-                nc.scalar.activation(
-                    out=squares[:, first_hi : first_hi + BANK_HI, 0:width],
-                    in_=product[:, :, 0:width],
-                    func=ACT.Square,
-                )
+            if first_hi == 0:
+                squares[i] = norm.tile([P, D_HI, GROUP], F32, name="squares", bufs=3)
+            product = multiply(i, first_hi)
+            nc.scalar.activation(
+                out=squares[i][:, first_hi : first_hi + BANK_HI, 0:width],
+                in_=product[:, :, 0:width],
+                func=ACT.Square,
+            )
+
+        def add_pairs(i):
+            width = width_of(i)
             pair_sums[i] = norm.tile([P, D_HI // 2, GROUP], F32, name="pair_sums", bufs=LAG_SUM + 2)
             nc.gpsimd.tensor_tensor(
                 out=pair_sums[i][:, :, 0:width],
-                in0=squares[:, 0:2, 0:width],
-                in1=squares[:, 2:4, 0:width],
+                in0=squares[i][:, 0:2, 0:width],
+                in1=squares[i][:, 2:4, 0:width],
                 op=ALU.add,
             )
 
         def finish_sum(i):
             width = width_of(i)
-            hi_sums[i] = norm.tile([P, GROUP], F32, name="hi_sums", bufs=LAG_NORM - LAG_SUM + 2)
+            hi_sums[i] = norm.tile([P, GROUP], F32, name="hi_sums", bufs=LAG_NORM - LAG_SUM + BUNCH + 1)
             nc.vector.tensor_tensor(
                 out=hi_sums[i][:, 0:width],
                 in0=pair_sums[i][:, 0, 0:width],
@@ -192,50 +198,55 @@ def tile_costvolumeattention17_pa_kernel(tc, x, q_w, k_w, out_0, out_1):
                 op=ALU.add,
             )
 
-        def invert_norm(i):
-            width = width_of(i)
-            head_sums = banks.tile([P, GROUP], F32, tag="bank")
-            nc.tensor.matmul(
-                out=head_sums[:, 0:width],
-                lhsT=ones_lo[:].rearrange("p h i -> p (h i)"),
-                rhs=hi_sums[i][:, 0:width],
-                start=True,
-                stop=True,
-            )
-            inv_norms[i] = norm.tile([P, GROUP], F32, name="inv_norm", bufs=LAG_SCALE - LAG_NORM + 2)
-            nc.scalar.activation(
-                out=inv_norms[i][:, 0:width], in_=head_sums[:, 0:width], func=ACT.Abs_reciprocal_sqrt
-            )
-
-        def store(name, frame, frame_tile, first, end):
-            for t in frames_fed(shifts[name], frame):
-                for j in range(D_HI):
-                    nc.sync.dma_start(out=outputs[name][t, j][:, :, first:end], in_=frame_tile[:, j, first:end])
-
-        def scale_and_store(i):
-            group, name, pieces = items[i]
-            if pieces[0][1] == pieces[0][0] * FRAME:
-                frame_tiles[name] = [frames.tile([P, D_HI, FRAME], F32, name="frame_" + name)]
-            if len(pieces) > 1:
-                frame_tiles[name].append(frames.tile([P, D_HI, FRAME], F32, name="frame_" + name))
-            for first_hi in range(0, D_HI, BANK_HI):
-                product = multiply(i, first_hi)
-                for frame_tile, (frame, start, end) in zip(frame_tiles[name], pieces):
-                    columns = slice(start - group * GROUP, end - group * GROUP)
-                    nc.vector.scalar_tensor_tensor(
-                        out=frame_tile[:, first_hi : first_hi + BANK_HI, start - frame * FRAME : end - frame * FRAME],
-                        in0=inv_norms[i][:, columns].unsqueeze(1).to_broadcast([P, BANK_HI, end - start]),
-                        scalar=MAX_INV_NORM,
-                        in1=product[:, :, columns],
-                        op0=ALU.min,
-                        op1=ALU.mult,
+        def invert_norms(bunch):
+            for first in range(0, len(bunch), BANK_SUMS):
+                head_sums = banks.tile([P, BANK_SUMS, GROUP], F32, tag="bank")
+                for slot, i in enumerate(bunch[first : first + BANK_SUMS]):
+                    nc.tensor.matmul(
+                        out=head_sums[:, slot, 0 : width_of(i)],
+                        lhsT=ones_lo[:].rearrange("p h i -> p (h i)"),
+                        rhs=hi_sums[i][:, 0 : width_of(i)],
+                        start=True,
+                        stop=True,
                     )
+                for slot, i in enumerate(bunch[first : first + BANK_SUMS]):
+                    inv_norms[i] = norm.tile([P, GROUP], F32, name="inv_norm", bufs=LAG_SCALE - LAG_NORM + 2)
+                    nc.scalar.activation(
+                        out=inv_norms[i][:, 0 : width_of(i)],
+                        in_=head_sums[:, slot, 0 : width_of(i)],
+                        func=ACT.Abs_reciprocal_sqrt,
+                    )
+
+        def scale(i, first_hi):
+            group, name, pieces = items[i]
+            if first_hi == 0:
+                for frame, start, end in pieces:
+                    if start == frame * FRAME:
+                        frame_tiles[name].append(frames.tile([P, D_HI, FRAME], F32, name="frame_" + name))
+            product = multiply(i, first_hi)
+            for frame_tile, (frame, start, end) in zip(frame_tiles[name], pieces):
+                columns = slice(start - group * GROUP, end - group * GROUP)
+                nc.vector.scalar_tensor_tensor(
+                    out=frame_tile[:, first_hi : first_hi + BANK_HI, start - frame * FRAME : end - frame * FRAME],
+                    in0=inv_norms[i][:, columns].unsqueeze(1).to_broadcast([P, BANK_HI, end - start]),
+                    scalar=MAX_INV_NORM,
+                    in1=product[:, :, columns],
+                    op0=ALU.min,
+                    op1=ALU.mult,
+                )
+
+        def store(i):
+            group, name, pieces = items[i]
             for frame_tile, (frame, start, end) in zip(list(frame_tiles[name]), pieces):
-                if frame == T - 1:
-                    store(name, frame, frame_tile, start - frame * FRAME, end - frame * FRAME)
-                elif end == (frame + 1) * FRAME:
-                    store(name, frame, frame_tile, 0, FRAME)
-                if end == (frame + 1) * FRAME:
+                complete = end == (frame + 1) * FRAME
+                first = start - frame * FRAME if frame == T - 1 else 0
+                if complete or frame == T - 1:
+                    for t in frames_fed(shifts[name], frame):
+                        nc.sync.dma_start(
+                            out=outputs[name][t][:, :, first : end - frame * FRAME],
+                            in_=frame_tile[:, :, first : end - frame * FRAME],
+                        )
+                if complete:
                     frame_tiles[name] = frame_tiles[name][1:]
 
         at_once = [job for job in jobs if job[3] == 0]
@@ -246,19 +257,29 @@ def tile_costvolumeattention17_pa_kernel(tc, x, q_w, k_w, out_0, out_1):
 
         waiting = []
         next_job = 0
+        inverted = 0
         for step in range(len(items) + LAG_SCALE):
-            if step < len(items):
-                for job, grouped in waiting:
-                    quantise(nc, grouped, job[1], job[2])
-                waiting = []
-                if next_job < len(later) and later[next_job][3] <= step + AHEAD:
-                    job = later[next_job]
-                    next_job += 1
-                    waiting = [(job, turn_rows(nc, banks, stage, identity, job[0]))]
-                square(step)
+            first_passes = step < len(items)
+            second_passes = 0 <= step - LAG_SCALE < len(items)
+            for job, grouped in waiting:
+                quantise(nc, grouped, job[1], job[2])
+            waiting = []
+            if next_job < len(later) and later[next_job][3] <= step + AHEAD:
+                job = later[next_job]
+                next_job += 1
+                waiting = [(job, turn_rows(nc, banks, stage, identity, job[0]))]
+            for first_hi in range(0, D_HI, BANK_HI):
+                if first_passes:
+                    square(step, first_hi)
+                if second_passes:
+                    scale(step - LAG_SCALE, first_hi)
+            if first_passes:
+                add_pairs(step)
+            if second_passes:
+                store(step - LAG_SCALE)
             if 0 <= step - LAG_SUM < len(items):
                 finish_sum(step - LAG_SUM)
-            if 0 <= step - LAG_NORM < len(items):
-                invert_norm(step - LAG_NORM)
-            if 0 <= step - LAG_SCALE < len(items):
-                scale_and_store(step - LAG_SCALE)
+            if step % BUNCH == BUNCH - 1:
+                bunch = list(range(inverted, min(step - LAG_NORM + 1, len(items))))
+                invert_norms(bunch)
+                inverted += len(bunch)

from contextlib import ExitStack

import concourse.mybir as mybir
from concourse.masks import make_identity

F32 = mybir.dt.float32
BF16 = mybir.dt.bfloat16
U32 = mybir.dt.uint32
U8 = mybir.dt.uint8
FP8X4 = mybir.dt.float8_e4m3fn_x4
ALU = mybir.AluOpType
ACT = mybir.ActivationFunctionType

P = 128
PACK = 4
HALVES = 2
C = 512
T = 8
FRAME = 784
TOKENS = T * FRAME
HEADS = 32
D_LO = 4
D_HI = 4
GROUP = 256
GROUPS = (TOKENS + GROUP - 1) // GROUP
BANK_HI = 2
BANK_SUMS = 2
BLOCK = 4
BLOCK_TOKENS = BLOCK * P
BLOCKS = (TOKENS + BLOCK_TOKENS - 1) // BLOCK_TOKENS
BANK_ROWS = 2
MAX_INV_NORM = 1.0e12
LAG_SUM = 2
LAG_NORM = 4
LAG_SCALE = 6
BUNCH = 2
AHEAD = 4
KEY_LEAD = 3

FLOPS = 2 * TOKENS * C * (2 * HEADS * D_LO * D_HI)


def turn_rows(nc, banks, stage, identity, rows):
    sets = rows.shape[1]
    grouped = stage.tile([P, BLOCK * P * PACK], BF16, align_bytes=64)
    grouped_words = grouped[:].bitcast(F32).rearrange("p (g r u) -> p g r u", r=P, u=HALVES)
    for first in range(0, sets, BANK_ROWS):
        count = min(BANK_ROWS, sets - first)
        turned = banks.tile([P, BANK_ROWS, HALVES, P], F32, tag="bank")
        for g in range(count):
            row_words = rows[:, first + g, :].bitcast(F32)
            for u in range(HALVES):
                nc.tensor.transpose(turned[:, g, u, :], row_words[:, u * P : (u + 1) * P], identity[:])
        copy_out = nc.vector.tensor_copy if (first // BANK_ROWS) % 2 == 0 else nc.scalar.copy
        copy_out(
            grouped_words[:, first : first + count],
            turned[:, 0:count].rearrange("p g u r -> p g r u"),
        )
    return grouped[:, 0 : sets * P * PACK]


def quantise(nc, grouped, codes, scales):
    nc.vector.quantize_mx(out=codes.bitcast(FP8X4), scales=scales, in_=grouped)


def frame_pieces(group):
    start = group * GROUP
    end = min(start + GROUP, TOKENS)
    return [
        (frame, max(start, frame * FRAME), min(end, (frame + 1) * FRAME))
        for frame in range(start // FRAME, (end - 1) // FRAME + 1)
    ]


def frames_fed(shift, frame):
    return [t for t in range(T) if min(t + shift, T - 1) == frame]


def tile_costvolumeattention17_pa_kernel(tc, x, q_w, k_w, out_0, out_1):
    nc = tc.nc
    with ExitStack() as ctx:
        keep = ctx.enter_context(tc.tile_pool(name="keep", bufs=1))
        loads = ctx.enter_context(tc.tile_pool(name="loads", bufs=BLOCKS))
        stage = ctx.enter_context(tc.tile_pool(name="stage", bufs=3))
        norm = ctx.enter_context(tc.tile_pool(name="norm", bufs=4))
        frames = ctx.enter_context(tc.tile_pool(name="frames", bufs=3))
        banks = ctx.enter_context(tc.psum_pool(name="banks", bufs=8))
        ctx.enter_context(tc.manual_schedule())

        w_codes = {}
        w_scales = {}
        for name in ("q", "k"):
            w_codes[name] = keep.tile([P, D_HI * P], U32, align_bytes=64, name="w_codes_" + name)
            w_scales[name] = keep.tile([P, D_HI * P], U8, align_bytes=64, name="w_scales_" + name)
        x_codes = keep.tile([P, TOKENS], U32, align_bytes=64)
        x_scales = keep.tile([P, TOKENS], U8, align_bytes=64)

        outputs = {
            "q": out_0.rearrange("(h t) d i j -> t h d (i j)", t=T),
            "k": out_1.rearrange("(h t) d i j -> t h d (i j)", t=T),
        }
        shifts = {"q": 0, "k": 1}

        items = []
        for last_frame in range(-KEY_LEAD, T):
            for name, lead in (("q", 0), ("k", KEY_LEAD)):
                for group in range(GROUPS):
                    pieces = [piece for piece in frame_pieces(group) if frames_fed(shifts[name], piece[0])]
                    if pieces and frame_pieces(group)[-1][0] == last_frame + lead:
                        items.append((group, name, pieces))

        x_rows = x[0].rearrange("(a p) c -> p a c", p=P)
        weights = {"q": q_w, "k": k_w}
        jobs = []
        seen = []
        for i, (group, name, pieces) in enumerate(items):
            if name not in seen:
                seen.append(name)
                w_rows = keep.tile([P, D_HI, C], BF16, name="w_rows_" + name)
                nc.sync.dma_start(out=w_rows[:], in_=weights[name].rearrange("(m j) c -> m j c", j=D_HI))
                jobs.append((w_rows, w_codes[name][:], w_scales[name][:], i))
            block = group * GROUP // BLOCK_TOKENS
            if block not in seen:
                seen.append(block)
                first = block * BLOCK
                count = min(BLOCK, TOKENS // P - first)
                x_block = loads.tile([P, count, C], BF16, tag="x_block")
                nc.sync.dma_start(out=x_block[:], in_=x_rows[:, first : first + count, :])
                columns = slice(first * P, (first + count) * P)
                jobs.append((x_block, x_codes[:, columns], x_scales[:, columns], i))

        identity = keep.tile([P, P], F32)
        make_identity(nc, identity[:])
        same_head = keep.tile([P, HEADS], F32)
        nc.vector.tensor_reduce(
            out=same_head[:],
            in_=identity[:].rearrange("p (h i) -> p h i", i=D_LO),
            axis=mybir.AxisListType.X,
            op=ALU.add,
        )
        ones_lo = keep.tile([P, HEADS, D_LO], F32)
        nc.vector.tensor_copy(out=ones_lo[:], in_=same_head[:].unsqueeze(2).to_broadcast([P, HEADS, D_LO]))

        squares = {}
        pair_sums = {}
        hi_sums = {}
        inv_norms = {}
        frame_tiles = {"q": [], "k": []}

        def width_of(i):
            return min(GROUP, TOKENS - items[i][0] * GROUP)

        def multiply(i, first_hi):
            group, name, pieces = items[i]
            tokens = slice(group * GROUP, group * GROUP + width_of(i))
            product = banks.tile([P, BANK_HI, GROUP], F32, tag="bank")
            for j in range(BANK_HI):
                channels = slice((first_hi + j) * P, (first_hi + j + 1) * P)
                nc.tensor.matmul_mx(
                    out=product[:, j, 0 : width_of(i)],
                    lhsT=w_codes[name][:, channels].bitcast(FP8X4),
                    lhsT_scale=w_scales[name][:, channels],
                    rhs=x_codes[:, tokens].bitcast(FP8X4),
                    rhs_scale=x_scales[:, tokens],
                    start=True,
                    stop=True,
                )
            return product

        def square(i, first_hi):
            width = width_of(i)
            if first_hi == 0:
                squares[i] = norm.tile([P, D_HI, GROUP], F32, name="squares", bufs=3)
            product = multiply(i, first_hi)
            nc.scalar.activation(
                out=squares[i][:, first_hi : first_hi + BANK_HI, 0:width],
                in_=product[:, :, 0:width],
                func=ACT.Square,
            )

        def add_pairs(i):
            width = width_of(i)
            pair_sums[i] = norm.tile([P, D_HI // 2, GROUP], F32, name="pair_sums", bufs=LAG_SUM + 2)
            nc.gpsimd.tensor_tensor(
                out=pair_sums[i][:, :, 0:width],
                in0=squares[i][:, 0:2, 0:width],
                in1=squares[i][:, 2:4, 0:width],
                op=ALU.add,
            )

        def finish_sum(i):
            width = width_of(i)
            hi_sums[i] = norm.tile([P, GROUP], F32, name="hi_sums", bufs=LAG_NORM - LAG_SUM + BUNCH + 1)
            nc.vector.tensor_tensor(
                out=hi_sums[i][:, 0:width],
                in0=pair_sums[i][:, 0, 0:width],
                in1=pair_sums[i][:, 1, 0:width],
                op=ALU.add,
            )

        def invert_norms(bunch):
            for first in range(0, len(bunch), BANK_SUMS):
                head_sums = banks.tile([P, BANK_SUMS, GROUP], F32, tag="bank")
                for slot, i in enumerate(bunch[first : first + BANK_SUMS]):
                    nc.tensor.matmul(
                        out=head_sums[:, slot, 0 : width_of(i)],
                        lhsT=ones_lo[:].rearrange("p h i -> p (h i)"),
                        rhs=hi_sums[i][:, 0 : width_of(i)],
                        start=True,
                        stop=True,
                    )
                for slot, i in enumerate(bunch[first : first + BANK_SUMS]):
                    inv_norms[i] = norm.tile([P, GROUP], F32, name="inv_norm", bufs=LAG_SCALE - LAG_NORM + 2)
                    nc.scalar.activation(
                        out=inv_norms[i][:, 0 : width_of(i)],
                        in_=head_sums[:, slot, 0 : width_of(i)],
                        func=ACT.Abs_reciprocal_sqrt,
                    )

        def scale(i, first_hi):
            group, name, pieces = items[i]
            if first_hi == 0:
                for frame, start, end in pieces:
                    if start == frame * FRAME:
                        frame_tiles[name].append(frames.tile([P, D_HI, FRAME], F32, name="frame_" + name))
            product = multiply(i, first_hi)
            for frame_tile, (frame, start, end) in zip(frame_tiles[name], pieces):
                columns = slice(start - group * GROUP, end - group * GROUP)
                nc.vector.scalar_tensor_tensor(
                    out=frame_tile[:, first_hi : first_hi + BANK_HI, start - frame * FRAME : end - frame * FRAME],
                    in0=inv_norms[i][:, columns].unsqueeze(1).to_broadcast([P, BANK_HI, end - start]),
                    scalar=MAX_INV_NORM,
                    in1=product[:, :, columns],
                    op0=ALU.min,
                    op1=ALU.mult,
                )

        def store(i):
            group, name, pieces = items[i]
            for frame_tile, (frame, start, end) in zip(list(frame_tiles[name]), pieces):
                complete = end == (frame + 1) * FRAME
                first = start - frame * FRAME if frame == T - 1 else 0
                if complete or frame == T - 1:
                    for t in frames_fed(shifts[name], frame):
                        nc.sync.dma_start(
                            out=outputs[name][t][:, :, first : end - frame * FRAME],
                            in_=frame_tile[:, :, first : end - frame * FRAME],
                        )
                if complete:
                    frame_tiles[name] = frame_tiles[name][1:]

        at_once = [job for job in jobs if job[3] == 0]
        turned_rows = [turn_rows(nc, banks, stage, identity, job[0]) for job in at_once]
        for job, grouped in zip(at_once, turned_rows):
            quantise(nc, grouped, job[1], job[2])
        later = [job for job in jobs if job[3] > 0]

        waiting = []
        next_job = 0
        inverted = 0
        for step in range(len(items) + LAG_SCALE):
            first_passes = step < len(items)
            second_passes = 0 <= step - LAG_SCALE < len(items)
            for job, grouped in waiting:
                quantise(nc, grouped, job[1], job[2])
            waiting = []
            if next_job < len(later) and later[next_job][3] <= step + AHEAD:
                job = later[next_job]
                next_job += 1
                waiting = [(job, turn_rows(nc, banks, stage, identity, job[0]))]
            for first_hi in range(0, D_HI, BANK_HI):
                if first_passes:
                    square(step, first_hi)
                if second_passes:
                    scale(step - LAG_SCALE, first_hi)
            if first_passes:
                add_pairs(step)
            if second_passes:
                store(step - LAG_SCALE)
            if 0 <= step - LAG_SUM < len(items):
                finish_sum(step - LAG_SUM)
            if step % BUNCH == BUNCH - 1:
                bunch = list(range(inverted, min(step - LAG_NORM + 1, len(items))))
                invert_norms(bunch)
                inverted += len(bunch)
